import numpy as np
import ml_dtypes


def mxq(x, axis, fmt="e4m3"):
    dtype, down = {"e4m3": (ml_dtypes.float8_e4m3fn, 7), "e5m2": (ml_dtypes.float8_e5m2, 14)}[fmt]
    v = np.moveaxis(np.asarray(x, np.float32).astype(ml_dtypes.bfloat16).astype(np.float64), axis, -1)
    blocks = v.reshape(v.shape[:-1] + (-1, 32))
    amax = np.abs(blocks).max(-1, keepdims=True)
    byte = np.maximum(np.where(amax > 0, np.frexp(amax)[1] - 1 + 127, 0) - down, 1)
    scale = np.exp2(byte - 127.0)
    codes = (blocks / scale).astype(np.float32).astype(dtype).astype(np.float64)
    return np.moveaxis((codes * scale).reshape(v.shape), -1, axis)


WIDE = False


def mx_kscale(k):
    if not WIDE:
        return np.ones(k)
    levels = np.array([10, -10, 5, -5, 0])
    if k % 512:
        return np.exp2(np.random.permutation(np.resize(levels, k // 32))).repeat(32)
    a = np.empty((k // 512, 16))
    for p in range(k // 512):
        a[p, :8] = np.random.permutation(np.resize(levels, 8))
        for g in range(8):
            far = levels[np.abs(levels - a[p, g]) >= 10]
            a[p, g + 8] = far[np.random.randint(len(far))]
    return np.exp2(a.ravel()).repeat(32)


BF16 = ml_dtypes.bfloat16


def bf(x):
    return np.asarray(x, np.float32).astype(BF16)


def f64(x):
    return np.asarray(x).astype(np.float64)


B, N, VD, QD, D, H, NG, P = 128, 36, 2048, 1024, 512, 2, 20, 64
DH = D // H


def setup_inputs():
    s = mx_kscale(D)
    return {"out_t": bf(np.random.standard_normal((B, N, H, D)) * 0.7 * s),
            "out_w": bf(np.random.standard_normal((H, D, DH)) / np.sqrt(D) / s[None, :, None]),
            "out_b": bf(np.random.standard_normal(D) * 0.3),
            "self_feat": bf(np.random.standard_normal((B, N, D)) * 0.9),
            "vis": bf(np.maximum(np.random.standard_normal((B, N, D)), 0.0))}


def reference(out_t, out_w, out_b, self_feat, vis):
    t = mxq(f64(out_t), 3, "e4m3").reshape(B * N, H, D).swapaxes(0, 1)
    nb = t @ mxq(f64(out_w), 1, "e4m3")
    neighbor = nb.swapaxes(0, 1).reshape(B, N, D) + f64(out_b)
    imp_rel = np.maximum(f64(self_feat) + neighbor, 0.0)
    return f64(vis) + imp_rel

@@ -1,0 +1,252 @@
+from contextlib import ExitStack
+
+import concourse.mybir as mybir
+from concourse.masks import make_identity
+
+F32 = mybir.dt.float32
+BF16 = mybir.dt.bfloat16
+U32 = mybir.dt.uint32
+U8 = mybir.dt.uint8
+FP8X4 = mybir.dt.float8_e4m3fn_x4
+ALU = mybir.AluOpType
+ACT = mybir.ActivationFunctionType
+
+P = 128
+NOBJ = 36
+HEADS = 2
+K = 512
+DH = 256
+D = 512
+GT = 4
+GROUPS = NOBJ // GT
+NCOL = GT * P
+
+FLOPS = 2 * P * NOBJ * HEADS * K * DH
+UNITS = GROUPS * HEADS
+FIRST_PE_ADD = 5
+X_CHUNKS = [[0], [1], [2], [3, 4], [5, 6], [7, 8]]
+SV_CHUNKS = [[0], [1], [2], [3, 4], [5, 6], [7, 8]]
+OUT_CHUNKS = [[0], [1, 2], [3, 4], [5, 6], [7], [8]]
+
+
+def pe_adds(unit, pair):
+    return (pair == 0 and unit >= FIRST_PE_ADD) or unit == UNITS - 1
+
+
+def tile_implicitrelationencoder_pb_t_kernel(tc, out_t, out_w, out_b, self_feat, vis, out):
+    nc = tc.nc
+    with ExitStack() as ctx:
+        const = ctx.enter_context(tc.tile_pool(name="const", bufs=1))
+        loads = ctx.enter_context(tc.tile_pool(name="loads", bufs=1))
+        gpool = ctx.enter_context(tc.tile_pool(name="gpool", bufs=2))
+        cpool = ctx.enter_context(tc.tile_pool(name="cpool", bufs=2))
+        upool = ctx.enter_context(tc.tile_pool(name="upool", bufs=4))
+        outs = ctx.enter_context(tc.tile_pool(name="outs", bufs=3))
+        psum_t = ctx.enter_context(tc.psum_pool(name="psum_t", bufs=2))
+        psum_a = ctx.enter_context(tc.psum_pool(name="psum_a", bufs=2))
+        psum_b = ctx.enter_context(tc.psum_pool(name="psum_b", bufs=4))
+        ctx.enter_context(tc.manual_schedule())
+
+        ident = const.tile([P, P], F32)
+        make_identity(nc, ident[:])
+        ident_bf = const.tile([P, P], BF16)
+        make_identity(nc, ident_bf[:])
+
+        x_tiles = {}
+        s_tiles = {}
+        v_tiles = {}
+        o_tiles = {}
+        grouped_tiles = {}
+        code_tiles = {}
+        u_tiles = {}
+        tb_tiles = {}
+
+        def load_x(chunk):
+            g0 = chunk[0]
+            rows = len(chunk) * GT
+            x = loads.tile([P, rows, HEADS, K], BF16, name="x%d" % g0)
+            for i, g in enumerate(chunk):
+                x_tiles[g] = x[:, i * GT : (i + 1) * GT]
+            if g0 == 0:
+                nc.sync.dma_start(out=x[:, :, 0, :], in_=out_t[:, 0:GT, 0, :])
+                nc.sync.dma_start(
+                    out=wraw[:].rearrange("q h t c -> q h (t c)"),
+                    in_=out_w.rearrange("h (q t) c -> q h (t c)", q=P, t=4),
+                )
+                nc.sync.dma_start(out=x[:, :, 1, :], in_=out_t[:, 0:GT, 1, :])
+                nc.sync.dma_start(out=bz[0:4, :], in_=out_b.rearrange("(j m) -> j m", j=4))
+            else:
+                nc.sync.dma_start(out=x[:], in_=out_t[:, g0 * GT : g0 * GT + rows])
+
+        def load_sv(chunk):
+            g0 = chunk[0]
+            rows = len(chunk) * GT
+            s = loads.tile([P, rows, D], BF16, name="s%d" % g0)
+            nc.sync.dma_start(out=s[:], in_=self_feat[:, g0 * GT : g0 * GT + rows, :])
+            v = loads.tile([P, rows, D], BF16, name="v%d" % g0)
+            nc.sync.dma_start(out=v[:], in_=vis[:, g0 * GT : g0 * GT + rows, :])
+            for i, g in enumerate(chunk):
+                s_tiles[g] = s[:, i * GT : (i + 1) * GT]
+                v_tiles[g] = v[:, i * GT : (i + 1) * GT]
+
+        def transpose_in(unit):
+            g, h = divmod(unit, HEADS)
+            xw = x_tiles[g].rearrange("p n h k -> p (n h k)").bitcast(F32)
+            grouped = gpool.tile([P, NCOL * 4], BF16, align_bytes=64, name="grouped", tag="grouped")
+            gw = grouped[:].bitcast(F32)
+            for pair in range(2):
+                xt = psum_t.tile([P, 2, 2, P], F32, name="xt", tag="xt")
+                for n2 in range(2):
+                    for u in range(2):
+                        c0 = ((pair * 2 + n2) * HEADS + h) * 256
+                        nc.tensor.transpose(xt[:, n2, u, :], xw[:, c0 + u : c0 + 256 : 2], ident[:])
+                nc.scalar.copy(
+                    out=gw[:, pair * 512 : (pair + 1) * 512].rearrange("q (n b u) -> q n b u", n=2, u=2),
+                    in_=xt[:].rearrange("q n u b -> q n b u"),
+                )
+            grouped_tiles[unit] = grouped
+
+        def quantise(unit):
+            codes = cpool.tile([P, NCOL], U32, align_bytes=64, name="codes", tag="codes")
+            scales = cpool.tile([P, NCOL], U8, align_bytes=64, name="scales", tag="scales")
+            nc.vector.quantize_mx(out=codes[:].bitcast(FP8X4), scales=scales[:], in_=grouped_tiles[unit][:])
+            code_tiles[unit] = (codes, scales)
+
+        def multiply(unit):
+            h = unit % HEADS
+            codes, scales = code_tiles[unit]
+            us = []
+            for j in range(2):
+                cb = h * 2 + j
+                acc = psum_a.tile([P, NCOL], F32, name="acc", tag="acc")
+                nc.tensor.matmul_mx(
+                    out=acc[:],
+                    lhsT=w_codes[:, cb * P : (cb + 1) * P].bitcast(FP8X4),
+                    lhsT_scale=w_scales[:, cb * P : (cb + 1) * P],
+                    rhs=codes[:].bitcast(FP8X4),
+                    rhs_scale=scales[:],
+                    start=True,
+                    stop=True,
+                )
+                u_sb = upool.tile([P, NCOL], F32, name="u_sb", tag="u")
+                nc.scalar.activation(
+                    out=u_sb[:], in_=acc[:], func=ACT.Identity, bias=bias_col[:, cb : cb + 1], scale=1.0
+                )
+                us.append(u_sb)
+            u_tiles[unit] = us
+
+        def transpose_back(unit):
+            g, h = divmod(unit, HEADS)
+            us = u_tiles[unit]
+            tbs = []
+            for pair in range(2):
+                tb = psum_b.tile([P, 2, DH], F32, name="tb", tag="tb")
+                for n2 in range(2):
+                    n = pair * 2 + n2
+                    if pe_adds(unit, pair):
+                        nc.tensor.matmul(
+                            out=tb[:, n2, :],
+                            lhsT=ident_bf[:],
+                            rhs=s_tiles[g][:, n, h * DH : (h + 1) * DH],
+                            start=True,
+                            stop=False,
+                        )
+                        for j in range(2):
+                            nc.tensor.matmul(
+                                out=tb[:, n2, j * P : (j + 1) * P],
+                                lhsT=us[j][:, n * P : (n + 1) * P],
+                                rhs=ident[:],
+                                is_transpose=True,
+                                start=False,
+                                stop=(j == 1),
+                            )
+                    else:
+                        for j in range(2):
+                            nc.tensor.transpose(tb[:, n2, j * P : (j + 1) * P], us[j][:, n * P : (n + 1) * P], ident[:])
+                tbs.append(tb)
+            tb_tiles[unit] = tbs
+
+        def finish(unit):
+            g, h = divmod(unit, HEADS)
+            chunk = [c for c in OUT_CHUNKS if g in c][0]
+            if h == 0 and g == chunk[0]:
+                whole = outs.tile([P, len(chunk) * GT, D], F32, name="o", tag="o")
+                for i, gg in enumerate(chunk):
+                    o_tiles[gg] = (whole[:, i * GT : (i + 1) * GT], whole)
+            o, whole = o_tiles[g]
+            v = v_tiles[g]
+            cols = slice(h * DH, (h + 1) * DH)
+            n0 = g * GT
+            plain = [pair for pair in range(2) if not pe_adds(unit, pair)]
+            for pair in range(2):
+                rows = slice(pair * 2, pair * 2 + 2)
+                if pe_adds(unit, pair):
+                    nc.vector.scalar_tensor_tensor(
+                        out=o[:, rows, cols], in0=tb_tiles[unit][pair][:], scalar=0.0, in1=v[:, rows, cols],
+                        op0=ALU.max, op1=ALU.add,
+                    )
+                    if unit == UNITS - 1:
+                        nc.sync.dma_start(out=out[:, n0 + pair * 2 : n0 + pair * 2 + 2, cols], in_=o[:, rows, cols])
+                else:
+                    nc.vector.tensor_tensor(
+                        out=o[:, rows, cols], in0=tb_tiles[unit][pair][:], in1=s_tiles[g][:, rows, cols], op=ALU.add
+                    )
+            if plain:
+                rest = slice(plain[0] * 2, GT)
+                nc.vector.scalar_tensor_tensor(
+                    out=o[:, rest, cols], in0=o[:, rest, cols], scalar=0.0, in1=v[:, rest, cols],
+                    op0=ALU.max, op1=ALU.add,
+                )
+            if g < GROUPS - 1:
+                if h == HEADS - 1 and g == chunk[-1]:
+                    nc.sync.dma_start(out=out[:, chunk[0] * GT : (g + 1) * GT, :], in_=whole[:])
+            elif unit < UNITS - 1:
+                nc.sync.dma_start(out=out[:, n0 : n0 + GT, cols], in_=o[:, :, cols])
+
+        wraw = const.tile([P, HEADS, 4, DH], BF16)
+        bz = const.tile([P, P], BF16)
+        nc.vector.memset(bz[:], 0.0)
+        load_plan = sorted(
+            [(2 * c[0] - 8, 0, c) for c in X_CHUNKS] + [(2 * c[0] - 5, 1, c) for c in SV_CHUNKS]
+        )
+
+        def trigger_loads(step):
+            for when, kind, chunk in load_plan:
+                if when == step or (step == 0 and when < 0):
+                    if kind == 0:
+                        load_x(chunk)
+                    else:
+                        load_sv(chunk)
+
+        trigger_loads(0)
+
+        wg = const.tile([P, HEADS, DH, 4], BF16, align_bytes=64)
+        w_codes = const.tile([P, HEADS * DH], U32, align_bytes=64)
+        w_scales = const.tile([P, HEADS * DH], U8, align_bytes=64)
+        for h in range(HEADS):
+            nc.vector.tensor_copy(out=wg[:, h], in_=wraw[:, h].rearrange("q t c -> q c t"))
+            nc.vector.quantize_mx(
+                out=w_codes[:, h * DH : (h + 1) * DH].bitcast(FP8X4),
+                scales=w_scales[:, h * DH : (h + 1) * DH],
+                in_=wg[:, h].rearrange("q c t -> q (c t)"),
+            )
+        bzf = const.tile([P, P], F32)
+        bias_col = const.tile([P, 4], F32)
+
+        for step in range(UNITS + 3):
+            if step > 0:
+                trigger_loads(step)
+            if step < UNITS:
+                transpose_in(step)
+            if step == 1:
+                nc.vector.tensor_copy(out=bzf[:], in_=bz[:])
+                bt = psum_b.tile([P, P], F32, name="bt", tag="tb")
+                nc.tensor.transpose(bt[:], bzf[:], ident[:])
+                nc.vector.tensor_copy(out=bias_col[:], in_=bt[:, 0:4])
+            if 0 <= step - 1 < UNITS:
+                quantise(step - 1)
+                multiply(step - 1)
+            if 0 <= step - 2 < UNITS:
+                transpose_back(step - 2)
+            if 0 <= step - 3 < UNITS:
+                finish(step - 3)

@@ -26,7 +26,7 @@ UNITS = GROUPS * HEADS
 FIRST_PE_ADD = 5
 X_CHUNKS = [[0], [1], [2], [3, 4], [5, 6], [7, 8]]
 SV_CHUNKS = [[0], [1], [2], [3, 4], [5, 6], [7, 8]]
-OUT_CHUNKS = [[0], [1, 2], [3, 4], [5, 6], [7], [8]]
+OUT_CHUNKS = [[0], [1], [2], [3, 4], [5, 6], [7], [8]]
 
 
 def pe_adds(unit, pair):
@@ -41,7 +41,6 @@ def tile_implicitrelationencoder_pb_t_kernel(tc, out_t, out_w, out_b, self_feat,
         gpool = ctx.enter_context(tc.tile_pool(name="gpool", bufs=2))
         cpool = ctx.enter_context(tc.tile_pool(name="cpool", bufs=2))
         upool = ctx.enter_context(tc.tile_pool(name="upool", bufs=4))
-        outs = ctx.enter_context(tc.tile_pool(name="outs", bufs=3))
         psum_t = ctx.enter_context(tc.psum_pool(name="psum_t", bufs=2))
         psum_a = ctx.enter_context(tc.psum_pool(name="psum_a", bufs=2))
         psum_b = ctx.enter_context(tc.psum_pool(name="psum_b", bufs=4))
@@ -52,10 +51,10 @@ def tile_implicitrelationencoder_pb_t_kernel(tc, out_t, out_w, out_b, self_feat,
         ident_bf = const.tile([P, P], BF16)
         make_identity(nc, ident_bf[:])
 
-        x_tiles = {}
+        xo_tiles = {}
+        xo_chunk = {}
         s_tiles = {}
         v_tiles = {}
-        o_tiles = {}
         grouped_tiles = {}
         code_tiles = {}
         u_tiles = {}
@@ -64,9 +63,11 @@ def tile_implicitrelationencoder_pb_t_kernel(tc, out_t, out_w, out_b, self_feat,
         def load_x(chunk):
             g0 = chunk[0]
             rows = len(chunk) * GT
-            x = loads.tile([P, rows, HEADS, K], BF16, name="x%d" % g0)
+            xo = loads.tile([P, rows, D], F32, name="xo%d" % g0)
+            x = xo[:].bitcast(BF16).rearrange("p n (h k) -> p n h k", h=HEADS)
             for i, g in enumerate(chunk):
-                x_tiles[g] = x[:, i * GT : (i + 1) * GT]
+                xo_tiles[g] = xo[:, i * GT : (i + 1) * GT]
+            xo_chunk[g0] = xo
             if g0 == 0:
                 nc.sync.dma_start(out=x[:, :, 0, :], in_=out_t[:, 0:GT, 0, :])
                 nc.sync.dma_start(
@@ -76,7 +77,7 @@ def tile_implicitrelationencoder_pb_t_kernel(tc, out_t, out_w, out_b, self_feat,
                 nc.sync.dma_start(out=x[:, :, 1, :], in_=out_t[:, 0:GT, 1, :])
                 nc.sync.dma_start(out=bz[0:4, :], in_=out_b.rearrange("(j m) -> j m", j=4))
             else:
-                nc.sync.dma_start(out=x[:], in_=out_t[:, g0 * GT : g0 * GT + rows])
+                nc.sync.dma_start(out=x, in_=out_t[:, g0 * GT : g0 * GT + rows])
 
         def load_sv(chunk):
             g0 = chunk[0]
@@ -91,7 +92,7 @@ def tile_implicitrelationencoder_pb_t_kernel(tc, out_t, out_w, out_b, self_feat,
 
         def transpose_in(unit):
             g, h = divmod(unit, HEADS)
-            xw = x_tiles[g].rearrange("p n h k -> p (n h k)").bitcast(F32)
+            xw = xo_tiles[g].rearrange("p n d -> p (n d)")
             grouped = gpool.tile([P, NCOL * 4], BF16, align_bytes=64, name="grouped", tag="grouped")
             gw = grouped[:].bitcast(F32)
             for pair in range(2):
@@ -169,11 +170,7 @@ def tile_implicitrelationencoder_pb_t_kernel(tc, out_t, out_w, out_b, self_feat,
         def finish(unit):
             g, h = divmod(unit, HEADS)
             chunk = [c for c in OUT_CHUNKS if g in c][0]
-            if h == 0 and g == chunk[0]:
-                whole = outs.tile([P, len(chunk) * GT, D], F32, name="o", tag="o")
-                for i, gg in enumerate(chunk):
-                    o_tiles[gg] = (whole[:, i * GT : (i + 1) * GT], whole)
-            o, whole = o_tiles[g]
+            o = xo_tiles[g]
             v = v_tiles[g]
             cols = slice(h * DH, (h + 1) * DH)
             n0 = g * GT
@@ -199,7 +196,9 @@ def tile_implicitrelationencoder_pb_t_kernel(tc, out_t, out_w, out_b, self_feat,
                 )
             if g < GROUPS - 1:
                 if h == HEADS - 1 and g == chunk[-1]:
-                    nc.sync.dma_start(out=out[:, chunk[0] * GT : (g + 1) * GT, :], in_=whole[:])
+                    nc.sync.dma_start(
+                        out=out[:, chunk[0] * GT : (g + 1) * GT, :], in_=xo_chunk[chunk[0]][:, 0 : len(chunk) * GT]
+                    )
             elif unit < UNITS - 1:
                 nc.sync.dma_start(out=out[:, n0 : n0 + GT, cols], in_=o[:, :, cols])
 
@@ -210,15 +209,11 @@ def tile_implicitrelationencoder_pb_t_kernel(tc, out_t, out_w, out_b, self_feat,
             [(2 * c[0] - 8, 0, c) for c in X_CHUNKS] + [(2 * c[0] - 5, 1, c) for c in SV_CHUNKS]
         )
 
-        def trigger_loads(step):
-            for when, kind, chunk in load_plan:
-                if when == step or (step == 0 and when < 0):
-                    if kind == 0:
-                        load_x(chunk)
-                    else:
-                        load_sv(chunk)
-
-        trigger_loads(0)
+        for when, kind, chunk in load_plan:
+            if kind == 0:
+                load_x(chunk)
+            else:
+                load_sv(chunk)
 
         wg = const.tile([P, HEADS, DH, 4], BF16, align_bytes=64)
         w_codes = const.tile([P, HEADS * DH], U32, align_bytes=64)
@@ -234,8 +229,6 @@ def tile_implicitrelationencoder_pb_t_kernel(tc, out_t, out_w, out_b, self_feat,
         bias_col = const.tile([P, 4], F32)
 
         for step in range(UNITS + 3):
-            if step > 0:
-                trigger_loads(step)
             if step < UNITS:
                 transpose_in(step)
             if step == 1:

@@ -24,9 +24,12 @@ NCOL = GT * P
 FLOPS = 2 * P * NOBJ * HEADS * K * DH
 UNITS = GROUPS * HEADS
 FIRST_PE_ADD = 5
-X_CHUNKS = [[0], [1], [2], [3, 4], [5, 6], [7, 8]]
-SV_CHUNKS = [[0], [1], [2], [3, 4], [5, 6], [7, 8]]
-OUT_CHUNKS = [[0], [1], [2], [3, 4], [5, 6], [7], [8]]
+X, SV = 0, 1
+LOAD_ORDER = [
+    (X, 0, 1), (X, 1, 2), (SV, 0, 1), (X, 2, 3), (SV, 1, 2), (X, 3, 5), (SV, 2, 3), (SV, 3, 5), (X, 5, 7), (SV, 5, 7),
+    (X, 7, 9), (SV, 7, 9),
+]
+OUT_CHUNKS = [(0, 1), (1, 2), (2, 3), (3, 5), (5, 7), (7, 8)]
 
 
 def pe_adds(unit, pair):
@@ -51,48 +54,38 @@ def tile_implicitrelationencoder_pb_t_kernel(tc, out_t, out_w, out_b, self_feat,
         ident_bf = const.tile([P, P], BF16)
         make_identity(nc, ident_bf[:])
 
-        xo_tiles = {}
-        xo_chunk = {}
-        s_tiles = {}
-        v_tiles = {}
         grouped_tiles = {}
         code_tiles = {}
         u_tiles = {}
         tb_tiles = {}
 
-        def load_x(chunk):
-            g0 = chunk[0]
-            rows = len(chunk) * GT
-            xo = loads.tile([P, rows, D], F32, name="xo%d" % g0)
-            x = xo[:].bitcast(BF16).rearrange("p n (h k) -> p n h k", h=HEADS)
-            for i, g in enumerate(chunk):
-                xo_tiles[g] = xo[:, i * GT : (i + 1) * GT]
-            xo_chunk[g0] = xo
-            if g0 == 0:
-                nc.sync.dma_start(out=x[:, :, 0, :], in_=out_t[:, 0:GT, 0, :])
+        xo = loads.tile([P, NOBJ, D], F32, name="xo")
+        s_all = loads.tile([P, NOBJ, D], BF16, name="s_all")
+        v_all = loads.tile([P, NOBJ, D], BF16, name="v_all")
+
+        def load(kind, g0, g1):
+            rows = slice(g0 * GT, g1 * GT)
+            if kind == SV:
+                nc.sync.dma_start(out=s_all[:, rows, :], in_=self_feat[:, rows, :])
+                nc.sync.dma_start(out=v_all[:, rows, :], in_=vis[:, rows, :])
+            elif g0 > 0:
+                nc.sync.dma_start(
+                    out=xo[:, rows, :].rearrange("p n d -> p (n d)").bitcast(BF16),
+                    in_=out_t[:, rows].rearrange("p n h k -> p (n h k)"),
+                )
+            else:
+                x0 = xo[:].bitcast(BF16).rearrange("p n (h k) -> p n h k", h=HEADS)
+                nc.sync.dma_start(out=x0[:, rows, 0, :], in_=out_t[:, rows, 0, :])
                 nc.sync.dma_start(
                     out=wraw[:].rearrange("q h t c -> q h (t c)"),
                     in_=out_w.rearrange("h (q t) c -> q h (t c)", q=P, t=4),
                 )
-                nc.sync.dma_start(out=x[:, :, 1, :], in_=out_t[:, 0:GT, 1, :])
+                nc.sync.dma_start(out=x0[:, rows, 1, :], in_=out_t[:, rows, 1, :])
                 nc.sync.dma_start(out=bz[0:4, :], in_=out_b.rearrange("(j m) -> j m", j=4))
-            else:
-                nc.sync.dma_start(out=x, in_=out_t[:, g0 * GT : g0 * GT + rows])
-
-        def load_sv(chunk):
-            g0 = chunk[0]
-            rows = len(chunk) * GT
-            s = loads.tile([P, rows, D], BF16, name="s%d" % g0)
-            nc.sync.dma_start(out=s[:], in_=self_feat[:, g0 * GT : g0 * GT + rows, :])
-            v = loads.tile([P, rows, D], BF16, name="v%d" % g0)
-            nc.sync.dma_start(out=v[:], in_=vis[:, g0 * GT : g0 * GT + rows, :])
-            for i, g in enumerate(chunk):
-                s_tiles[g] = s[:, i * GT : (i + 1) * GT]
-                v_tiles[g] = v[:, i * GT : (i + 1) * GT]
 
         def transpose_in(unit):
             g, h = divmod(unit, HEADS)
-            xw = xo_tiles[g].rearrange("p n d -> p (n d)")
+            xw = xo[:, g * GT : (g + 1) * GT, :].rearrange("p n d -> p (n d)")
             grouped = gpool.tile([P, NCOL * 4], BF16, align_bytes=64, name="grouped", tag="grouped")
             gw = grouped[:].bitcast(F32)
             for pair in range(2):
@@ -142,78 +135,63 @@ def tile_implicitrelationencoder_pb_t_kernel(tc, out_t, out_w, out_b, self_feat,
             tbs = []
             for pair in range(2):
                 tb = psum_b.tile([P, 2, DH], F32, name="tb", tag="tb")
+                tbs.append(tb)
+                if pe_adds(unit, pair):
+                    n0 = g * GT + pair * 2
+                    nc.tensor.matmul(
+                        out=tb[:],
+                        lhsT=ident_bf[:],
+                        rhs=s_all[:, n0 : n0 + 2, h * DH : (h + 1) * DH],
+                        start=True,
+                        stop=False,
+                    )
+            for pair in range(2):
                 for n2 in range(2):
                     n = pair * 2 + n2
-                    if pe_adds(unit, pair):
+                    for j in range(2):
+                        first = not pe_adds(unit, pair)
                         nc.tensor.matmul(
-                            out=tb[:, n2, :],
-                            lhsT=ident_bf[:],
-                            rhs=s_tiles[g][:, n, h * DH : (h + 1) * DH],
-                            start=True,
-                            stop=False,
+                            out=tbs[pair][:, n2, j * P : (j + 1) * P],
+                            lhsT=us[j][:, n * P : (n + 1) * P],
+                            rhs=ident[:],
+                            is_transpose=True,
+                            start=first,
+                            stop=first or (n2 == 1 and j == 1),
                         )
-                        for j in range(2):
-                            nc.tensor.matmul(
-                                out=tb[:, n2, j * P : (j + 1) * P],
-                                lhsT=us[j][:, n * P : (n + 1) * P],
-                                rhs=ident[:],
-                                is_transpose=True,
-                                start=False,
-                                stop=(j == 1),
-                            )
-                    else:
-                        for j in range(2):
-                            nc.tensor.transpose(tb[:, n2, j * P : (j + 1) * P], us[j][:, n * P : (n + 1) * P], ident[:])
-                tbs.append(tb)
             tb_tiles[unit] = tbs
 
         def finish(unit):
             g, h = divmod(unit, HEADS)
-            chunk = [c for c in OUT_CHUNKS if g in c][0]
-            o = xo_tiles[g]
-            v = v_tiles[g]
+            o = xo[:, g * GT : (g + 1) * GT, :]
+            s = s_all[:, g * GT : (g + 1) * GT, :]
+            v = v_all[:, g * GT : (g + 1) * GT, :]
             cols = slice(h * DH, (h + 1) * DH)
             n0 = g * GT
+            tbs = tb_tiles[unit]
             plain = [pair for pair in range(2) if not pe_adds(unit, pair)]
+            for pair in plain:
+                rows = slice(pair * 2, pair * 2 + 2)
+                nc.vector.tensor_tensor(out=o[:, rows, cols], in0=tbs[pair][:], in1=s[:, rows, cols], op=ALU.add)
             for pair in range(2):
                 rows = slice(pair * 2, pair * 2 + 2)
-                if pe_adds(unit, pair):
-                    nc.vector.scalar_tensor_tensor(
-                        out=o[:, rows, cols], in0=tb_tiles[unit][pair][:], scalar=0.0, in1=v[:, rows, cols],
-                        op0=ALU.max, op1=ALU.add,
-                    )
-                    if unit == UNITS - 1:
-                        nc.sync.dma_start(out=out[:, n0 + pair * 2 : n0 + pair * 2 + 2, cols], in_=o[:, rows, cols])
-                else:
-                    nc.vector.tensor_tensor(
-                        out=o[:, rows, cols], in0=tb_tiles[unit][pair][:], in1=s_tiles[g][:, rows, cols], op=ALU.add
-                    )
-            if plain:
-                rest = slice(plain[0] * 2, GT)
                 nc.vector.scalar_tensor_tensor(
-                    out=o[:, rest, cols], in0=o[:, rest, cols], scalar=0.0, in1=v[:, rest, cols],
-                    op0=ALU.max, op1=ALU.add,
+                    out=o[:, rows, cols], in0=o[:, rows, cols] if pair in plain else tbs[pair][:], scalar=0.0,
+                    in1=v[:, rows, cols], op0=ALU.max, op1=ALU.add,
                 )
+                if unit == UNITS - 1:
+                    nc.sync.dma_start(out=out[:, n0 + pair * 2 : n0 + pair * 2 + 2, cols], in_=o[:, rows, cols])
             if g < GROUPS - 1:
-                if h == HEADS - 1 and g == chunk[-1]:
-                    nc.sync.dma_start(
-                        out=out[:, chunk[0] * GT : (g + 1) * GT, :], in_=xo_chunk[chunk[0]][:, 0 : len(chunk) * GT]
-                    )
+                for g0, g1 in OUT_CHUNKS:
+                    if h == HEADS - 1 and g == g1 - 1:
+                        nc.sync.dma_start(out=out[:, g0 * GT : g1 * GT, :], in_=xo[:, g0 * GT : g1 * GT, :])
             elif unit < UNITS - 1:
                 nc.sync.dma_start(out=out[:, n0 : n0 + GT, cols], in_=o[:, :, cols])
 
         wraw = const.tile([P, HEADS, 4, DH], BF16)
         bz = const.tile([P, P], BF16)
         nc.vector.memset(bz[:], 0.0)
-        load_plan = sorted(
-            [(2 * c[0] - 8, 0, c) for c in X_CHUNKS] + [(2 * c[0] - 5, 1, c) for c in SV_CHUNKS]
-        )
-
-        for when, kind, chunk in load_plan:
-            if kind == 0:
-                load_x(chunk)
-            else:
-                load_sv(chunk)
+        for kind, g0, g1 in LOAD_ORDER:
+            load(kind, g0, g1)
 
         wg = const.tile([P, HEADS, DH, 4], BF16, align_bytes=64)
         w_codes = const.tile([P, HEADS * DH], U32, align_bytes=64)

@@ -135,29 +135,29 @@ def tile_implicitrelationencoder_pb_t_kernel(tc, out_t, out_w, out_b, self_feat,
             tbs = []
             for pair in range(2):
                 tb = psum_b.tile([P, 2, DH], F32, name="tb", tag="tb")
-                tbs.append(tb)
-                if pe_adds(unit, pair):
-                    n0 = g * GT + pair * 2
-                    nc.tensor.matmul(
-                        out=tb[:],
-                        lhsT=ident_bf[:],
-                        rhs=s_all[:, n0 : n0 + 2, h * DH : (h + 1) * DH],
-                        start=True,
-                        stop=False,
-                    )
-            for pair in range(2):
                 for n2 in range(2):
                     n = pair * 2 + n2
-                    for j in range(2):
-                        first = not pe_adds(unit, pair)
+                    if pe_adds(unit, pair):
                         nc.tensor.matmul(
-                            out=tbs[pair][:, n2, j * P : (j + 1) * P],
-                            lhsT=us[j][:, n * P : (n + 1) * P],
-                            rhs=ident[:],
-                            is_transpose=True,
-                            start=first,
-                            stop=first or (n2 == 1 and j == 1),
+                            out=tb[:, n2, :],
+                            lhsT=ident_bf[:],
+                            rhs=s_all[:, g * GT + n, h * DH : (h + 1) * DH],
+                            start=True,
+                            stop=False,
                         )
+                        for j in range(2):
+                            nc.tensor.matmul(
+                                out=tb[:, n2, j * P : (j + 1) * P],
+                                lhsT=us[j][:, n * P : (n + 1) * P],
+                                rhs=ident[:],
+                                is_transpose=True,
+                                start=False,
+                                stop=(j == 1),
+                            )
+                    else:
+                        for j in range(2):
+                            nc.tensor.transpose(tb[:, n2, j * P : (j + 1) * P], us[j][:, n * P : (n + 1) * P], ident[:])
+                tbs.append(tb)
             tb_tiles[unit] = tbs
 
         def finish(unit):

@@ -26,10 +26,9 @@ UNITS = GROUPS * HEADS
 FIRST_PE_ADD = 5
 X, SV = 0, 1
 LOAD_ORDER = [
-    (X, 0, 1), (X, 1, 2), (SV, 0, 1), (X, 2, 3), (SV, 1, 2), (X, 3, 5), (SV, 2, 3), (SV, 3, 5), (X, 5, 7), (SV, 5, 7),
-    (X, 7, 9), (SV, 7, 9),
+    (X, 0, 1), (X, 1, 2), (SV, 0, 1), (X, 2, 3), (SV, 1, 3), (X, 3, 5), (SV, 3, 6), (X, 5, 7), (X, 7, 9), (SV, 6, 9),
 ]
-OUT_CHUNKS = [(0, 1), (1, 2), (2, 3), (3, 5), (5, 7), (7, 8)]
+OUT_CHUNKS = [(0, 5), (5, 7), (7, 8), (8, 9)]
 
 
 def pe_adds(unit, pair):
@@ -74,13 +73,15 @@ def tile_implicitrelationencoder_pb_t_kernel(tc, out_t, out_w, out_b, self_feat,
                     in_=out_t[:, rows].rearrange("p n h k -> p (n h k)"),
                 )
             else:
-                x0 = xo[:].bitcast(BF16).rearrange("p n (h k) -> p n h k", h=HEADS)
-                nc.sync.dma_start(out=x0[:, rows, 0, :], in_=out_t[:, rows, 0, :])
+                for n0 in (0, 2):
+                    nc.sync.dma_start(
+                        out=xo[:, n0 : n0 + 2, :].rearrange("p n d -> p (n d)").bitcast(BF16),
+                        in_=out_t[:, n0 : n0 + 2].rearrange("p n h k -> p (n h k)"),
+                    )
                 nc.sync.dma_start(
                     out=wraw[:].rearrange("q h t c -> q h (t c)"),
                     in_=out_w.rearrange("h (q t) c -> q h (t c)", q=P, t=4),
                 )
-                nc.sync.dma_start(out=x0[:, rows, 1, :], in_=out_t[:, rows, 1, :])
                 nc.sync.dma_start(out=bz[0:4, :], in_=out_b.rearrange("(j m) -> j m", j=4))
 
         def transpose_in(unit):
@@ -166,7 +167,6 @@ def tile_implicitrelationencoder_pb_t_kernel(tc, out_t, out_w, out_b, self_feat,
             s = s_all[:, g * GT : (g + 1) * GT, :]
             v = v_all[:, g * GT : (g + 1) * GT, :]
             cols = slice(h * DH, (h + 1) * DH)
-            n0 = g * GT
             tbs = tb_tiles[unit]
             plain = [pair for pair in range(2) if not pe_adds(unit, pair)]
             for pair in plain:
@@ -178,14 +178,9 @@ def tile_implicitrelationencoder_pb_t_kernel(tc, out_t, out_w, out_b, self_feat,
                     out=o[:, rows, cols], in0=o[:, rows, cols] if pair in plain else tbs[pair][:], scalar=0.0,
                     in1=v[:, rows, cols], op0=ALU.max, op1=ALU.add,
                 )
-                if unit == UNITS - 1:
-                    nc.sync.dma_start(out=out[:, n0 + pair * 2 : n0 + pair * 2 + 2, cols], in_=o[:, rows, cols])
-            if g < GROUPS - 1:
-                for g0, g1 in OUT_CHUNKS:
-                    if h == HEADS - 1 and g == g1 - 1:
-                        nc.sync.dma_start(out=out[:, g0 * GT : g1 * GT, :], in_=xo[:, g0 * GT : g1 * GT, :])
-            elif unit < UNITS - 1:
-                nc.sync.dma_start(out=out[:, n0 : n0 + GT, cols], in_=o[:, :, cols])
+            for g0, g1 in OUT_CHUNKS:
+                if h == HEADS - 1 and g == g1 - 1:
+                    nc.sync.dma_start(out=out[:, g0 * GT : g1 * GT, :], in_=xo[:, g0 * GT : g1 * GT, :])
 
         wraw = const.tile([P, HEADS, 4, DH], BF16)
         bz = const.tile([P, P], BF16)

@@ -28,7 +28,7 @@ X, SV = 0, 1
 LOAD_ORDER = [
     (X, 0, 1), (X, 1, 2), (SV, 0, 1), (X, 2, 3), (SV, 1, 3), (X, 3, 5), (SV, 3, 6), (X, 5, 7), (X, 7, 9), (SV, 6, 9),
 ]
-OUT_CHUNKS = [(0, 5), (5, 7), (7, 8), (8, 9)]
+OUT_CHUNKS = [(0, 3), (3, 5), (5, 6), (6, 7), (7, 8)]
 
 
 def pe_adds(unit, pair):
@@ -178,6 +178,8 @@ def tile_implicitrelationencoder_pb_t_kernel(tc, out_t, out_w, out_b, self_feat,
                     out=o[:, rows, cols], in0=o[:, rows, cols] if pair in plain else tbs[pair][:], scalar=0.0,
                     in1=v[:, rows, cols], op0=ALU.max, op1=ALU.add,
                 )
+                if unit == UNITS - 1:
+                    nc.sync.dma_start(out=out[:, g * GT + pair * 2 : g * GT + pair * 2 + 2, :], in_=o[:, rows, :])
             for g0, g1 in OUT_CHUNKS:
                 if h == HEADS - 1 and g == g1 - 1:
                     nc.sync.dma_start(out=out[:, g0 * GT : g1 * GT, :], in_=xo[:, g0 * GT : g1 * GT, :])

@@ -24,15 +24,24 @@ NCOL = GT * P
 FLOPS = 2 * P * NOBJ * HEADS * K * DH
 UNITS = GROUPS * HEADS
 FIRST_PE_ADD = 5
+SPLIT_UNITS = range(1, 5)
 X, SV = 0, 1
 LOAD_ORDER = [
-    (X, 0, 1), (X, 1, 2), (SV, 0, 1), (X, 2, 3), (SV, 1, 3), (X, 3, 5), (SV, 3, 6), (X, 5, 7), (X, 7, 9), (SV, 6, 9),
+    (X, 0, 1), (X, 1, 2), (SV, 0, 1), (X, 2, 3), (SV, 1, 3), (X, 3, 5), (SV, 3, 6), (X, 5, 6), (X, 6, 9), (SV, 6, 9),
 ]
-OUT_CHUNKS = [(0, 3), (3, 5), (5, 6), (6, 7), (7, 8)]
+OUT_CHUNKS = [(0, 1), (1, 3), (3, 6), (6, 7), (7, 8)]
+BLOCKS = [(0, 1), (1, 3), (3, 6), (6, 9)]
 
 
 def pe_adds(unit, pair):
     return (pair == 0 and unit >= FIRST_PE_ADD) or unit == UNITS - 1
+
+
+def rows_of(tensor, g0, g1):
+    flat = tensor.rearrange("b n h k -> (b n) (h k)") if len(tensor.shape) == 4 else tensor.rearrange("b n d -> (b n) d")
+    a, b = [block for block in BLOCKS if block[0] <= g0 and g1 <= block[1]][0]
+    view = flat[a * GT * P : b * GT * P, :].rearrange("(p r) w -> p r w", p=P)
+    return view[:, (g0 - a) * GT : (g1 - a) * GT, :]
 
 
 def tile_implicitrelationencoder_pb_t_kernel(tc, out_t, out_w, out_b, self_feat, vis, out):
@@ -43,6 +52,7 @@ def tile_implicitrelationencoder_pb_t_kernel(tc, out_t, out_w, out_b, self_feat,
         gpool = ctx.enter_context(tc.tile_pool(name="gpool", bufs=2))
         cpool = ctx.enter_context(tc.tile_pool(name="cpool", bufs=2))
         upool = ctx.enter_context(tc.tile_pool(name="upool", bufs=4))
+        xpool = ctx.enter_context(tc.tile_pool(name="xpool", bufs=2))
         psum_t = ctx.enter_context(tc.psum_pool(name="psum_t", bufs=2))
         psum_a = ctx.enter_context(tc.psum_pool(name="psum_a", bufs=2))
         psum_b = ctx.enter_context(tc.psum_pool(name="psum_b", bufs=4))
@@ -53,6 +63,7 @@ def tile_implicitrelationencoder_pb_t_kernel(tc, out_t, out_w, out_b, self_feat,
         ident_bf = const.tile([P, P], BF16)
         make_identity(nc, ident_bf[:])
 
+        split_tiles = {}
         grouped_tiles = {}
         code_tiles = {}
         u_tiles = {}
@@ -65,24 +76,29 @@ def tile_implicitrelationencoder_pb_t_kernel(tc, out_t, out_w, out_b, self_feat,
         def load(kind, g0, g1):
             rows = slice(g0 * GT, g1 * GT)
             if kind == SV:
-                nc.sync.dma_start(out=s_all[:, rows, :], in_=self_feat[:, rows, :])
-                nc.sync.dma_start(out=v_all[:, rows, :], in_=vis[:, rows, :])
+                nc.sync.dma_start(out=s_all[:, rows, :], in_=rows_of(self_feat, g0, g1))
+                nc.sync.dma_start(out=v_all[:, rows, :], in_=rows_of(vis, g0, g1))
             elif g0 > 0:
-                nc.sync.dma_start(
-                    out=xo[:, rows, :].rearrange("p n d -> p (n d)").bitcast(BF16),
-                    in_=out_t[:, rows].rearrange("p n h k -> p (n h k)"),
-                )
+                nc.sync.dma_start(out=xo[:, rows, :].bitcast(BF16), in_=rows_of(out_t, g0, g1))
             else:
                 for n0 in (0, 2):
                     nc.sync.dma_start(
-                        out=xo[:, n0 : n0 + 2, :].rearrange("p n d -> p (n d)").bitcast(BF16),
-                        in_=out_t[:, n0 : n0 + 2].rearrange("p n h k -> p (n h k)"),
+                        out=xo[:, n0 : n0 + 2, :].bitcast(BF16), in_=rows_of(out_t, 0, 1)[:, n0 : n0 + 2, :]
                     )
                 nc.sync.dma_start(
                     out=wraw[:].rearrange("q h t c -> q h (t c)"),
                     in_=out_w.rearrange("h (q t) c -> q h (t c)", q=P, t=4),
                 )
                 nc.sync.dma_start(out=bz[0:4, :], in_=out_b.rearrange("(j m) -> j m", j=4))
+
+        def split_words(unit):
+            g, h = divmod(unit, HEADS)
+            split = xpool.tile([P, GT, 2, P], F32, name="split", tag="split")
+            nc.vector.tensor_copy(
+                out=split[:],
+                in_=xo[:, g * GT : (g + 1) * GT, h * DH : (h + 1) * DH].rearrange("p n (q u) -> p n u q", u=2),
+            )
+            split_tiles[unit] = split
 
         def transpose_in(unit):
             g, h = divmod(unit, HEADS)
@@ -94,7 +110,11 @@ def tile_implicitrelationencoder_pb_t_kernel(tc, out_t, out_w, out_b, self_feat,
                 for n2 in range(2):
                     for u in range(2):
                         c0 = ((pair * 2 + n2) * HEADS + h) * 256
-                        nc.tensor.transpose(xt[:, n2, u, :], xw[:, c0 + u : c0 + 256 : 2], ident[:])
+                        if unit in SPLIT_UNITS:
+                            words = split_tiles[unit][:, pair * 2 + n2, u, :]
+                        else:
+                            words = xw[:, c0 + u : c0 + 256 : 2]
+                        nc.tensor.transpose(xt[:, n2, u, :], words, ident[:])
                 nc.scalar.copy(
                     out=gw[:, pair * 512 : (pair + 1) * 512].rearrange("q (n b u) -> q n b u", n=2, u=2),
                     in_=xt[:].rearrange("q n u b -> q n b u"),
@@ -179,10 +199,10 @@ def tile_implicitrelationencoder_pb_t_kernel(tc, out_t, out_w, out_b, self_feat,
                     in1=v[:, rows, cols], op0=ALU.max, op1=ALU.add,
                 )
                 if unit == UNITS - 1:
-                    nc.sync.dma_start(out=out[:, g * GT + pair * 2 : g * GT + pair * 2 + 2, :], in_=o[:, rows, :])
+                    nc.sync.dma_start(out=rows_of(out, g, g + 1)[:, rows, :], in_=o[:, rows, :])
             for g0, g1 in OUT_CHUNKS:
                 if h == HEADS - 1 and g == g1 - 1:
-                    nc.sync.dma_start(out=out[:, g0 * GT : g1 * GT, :], in_=xo[:, g0 * GT : g1 * GT, :])
+                    nc.sync.dma_start(out=rows_of(out, g0, g1), in_=xo[:, g0 * GT : g1 * GT, :])
 
         wraw = const.tile([P, HEADS, 4, DH], BF16)
         bz = const.tile([P, P], BF16)
@@ -190,6 +210,7 @@ def tile_implicitrelationencoder_pb_t_kernel(tc, out_t, out_w, out_b, self_feat,
         for kind, g0, g1 in LOAD_ORDER:
             load(kind, g0, g1)
 
+        split_words(1)
         wg = const.tile([P, HEADS, DH, 4], BF16, align_bytes=64)
         w_codes = const.tile([P, HEADS * DH], U32, align_bytes=64)
         w_scales = const.tile([P, HEADS * DH], U8, align_bytes=64)
@@ -213,6 +234,8 @@ def tile_implicitrelationencoder_pb_t_kernel(tc, out_t, out_w, out_b, self_feat,
                 nc.vector.tensor_copy(out=bias_col[:], in_=bt[:, 0:4])
             if 0 <= step - 1 < UNITS:
                 quantise(step - 1)
+                if step + 1 in SPLIT_UNITS:
+                    split_words(step + 1)
                 multiply(step - 1)
             if 0 <= step - 2 < UNITS:
                 transpose_back(step - 2)

from contextlib import ExitStack

import concourse.mybir as mybir
from concourse.masks import make_identity

F32 = mybir.dt.float32
BF16 = mybir.dt.bfloat16
U32 = mybir.dt.uint32
U8 = mybir.dt.uint8
FP8X4 = mybir.dt.float8_e4m3fn_x4
ALU = mybir.AluOpType
ACT = mybir.ActivationFunctionType

P = 128
NOBJ = 36
HEADS = 2
K = 512
DH = 256
D = 512
GT = 4
GROUPS = NOBJ // GT
NCOL = GT * P

FLOPS = 2 * P * NOBJ * HEADS * K * DH
UNITS = GROUPS * HEADS
FIRST_PE_ADD = 5
SPLIT_UNITS = range(1, 5)
X, SV = 0, 1
LOAD_ORDER = [
    (X, 0, 1), (X, 1, 2), (SV, 0, 1), (X, 2, 3), (SV, 1, 3), (X, 3, 5), (SV, 3, 6), (X, 5, 6), (X, 6, 9), (SV, 6, 9),
]
OUT_CHUNKS = [(0, 1), (1, 3), (3, 6), (6, 7), (7, 8)]
BLOCKS = [(0, 1), (1, 3), (3, 6), (6, 9)]


def pe_adds(unit, pair):
    return (pair == 0 and unit >= FIRST_PE_ADD) or unit == UNITS - 1


def rows_of(tensor, g0, g1):
    flat = tensor.rearrange("b n h k -> (b n) (h k)") if len(tensor.shape) == 4 else tensor.rearrange("b n d -> (b n) d")
    a, b = [block for block in BLOCKS if block[0] <= g0 and g1 <= block[1]][0]
    view = flat[a * GT * P : b * GT * P, :].rearrange("(p r) w -> p r w", p=P)
    return view[:, (g0 - a) * GT : (g1 - a) * GT, :]


def tile_implicitrelationencoder_pb_t_kernel(tc, out_t, out_w, out_b, self_feat, vis, out):
    nc = tc.nc
    with ExitStack() as ctx:
        const = ctx.enter_context(tc.tile_pool(name="const", bufs=1))
        loads = ctx.enter_context(tc.tile_pool(name="loads", bufs=1))
        gpool = ctx.enter_context(tc.tile_pool(name="gpool", bufs=2))
        cpool = ctx.enter_context(tc.tile_pool(name="cpool", bufs=2))
        upool = ctx.enter_context(tc.tile_pool(name="upool", bufs=4))
        xpool = ctx.enter_context(tc.tile_pool(name="xpool", bufs=2))
        psum_t = ctx.enter_context(tc.psum_pool(name="psum_t", bufs=2))
        psum_a = ctx.enter_context(tc.psum_pool(name="psum_a", bufs=2))
        psum_b = ctx.enter_context(tc.psum_pool(name="psum_b", bufs=4))
        ctx.enter_context(tc.manual_schedule())

        ident = const.tile([P, P], F32)
        make_identity(nc, ident[:])
        ident_bf = const.tile([P, P], BF16)
        make_identity(nc, ident_bf[:])

        split_tiles = {}
        grouped_tiles = {}
        code_tiles = {}
        u_tiles = {}
        tb_tiles = {}

        xo = loads.tile([P, NOBJ, D], F32, name="xo")
        s_all = loads.tile([P, NOBJ, D], BF16, name="s_all")
        v_all = loads.tile([P, NOBJ, D], BF16, name="v_all")

        def load(kind, g0, g1):
            rows = slice(g0 * GT, g1 * GT)
            if kind == SV:
                nc.sync.dma_start(out=s_all[:, rows, :], in_=rows_of(self_feat, g0, g1))
                nc.sync.dma_start(out=v_all[:, rows, :], in_=rows_of(vis, g0, g1))
            elif g0 > 0:
                nc.sync.dma_start(out=xo[:, rows, :].bitcast(BF16), in_=rows_of(out_t, g0, g1))
            else:
                for n0 in (0, 2):
                    nc.sync.dma_start(
                        out=xo[:, n0 : n0 + 2, :].bitcast(BF16), in_=rows_of(out_t, 0, 1)[:, n0 : n0 + 2, :]
                    )
                nc.sync.dma_start(
                    out=wraw[:].rearrange("q h t c -> q h (t c)"),
                    in_=out_w.rearrange("h (q t) c -> q h (t c)", q=P, t=4),
                )
                nc.sync.dma_start(out=bz[0:4, :], in_=out_b.rearrange("(j m) -> j m", j=4))

        def split_words(unit):
            g, h = divmod(unit, HEADS)
            split = xpool.tile([P, GT, 2, P], F32, name="split", tag="split")
            nc.vector.tensor_copy(
                out=split[:],
                in_=xo[:, g * GT : (g + 1) * GT, h * DH : (h + 1) * DH].rearrange("p n (q u) -> p n u q", u=2),
            )
            split_tiles[unit] = split

        def transpose_in(unit):
            g, h = divmod(unit, HEADS)
            xw = xo[:, g * GT : (g + 1) * GT, :].rearrange("p n d -> p (n d)")
            grouped = gpool.tile([P, NCOL * 4], BF16, align_bytes=64, name="grouped", tag="grouped")
            gw = grouped[:].bitcast(F32)
            for pair in range(2):
                xt = psum_t.tile([P, 2, 2, P], F32, name="xt", tag="xt")
                for n2 in range(2):
                    for u in range(2):
                        c0 = ((pair * 2 + n2) * HEADS + h) * 256
                        if unit in SPLIT_UNITS:
                            words = split_tiles[unit][:, pair * 2 + n2, u, :]
                        else:
                            words = xw[:, c0 + u : c0 + 256 : 2]
                        nc.tensor.transpose(xt[:, n2, u, :], words, ident[:])
                nc.scalar.copy(
                    out=gw[:, pair * 512 : (pair + 1) * 512].rearrange("q (n b u) -> q n b u", n=2, u=2),
                    in_=xt[:].rearrange("q n u b -> q n b u"),
                )
            grouped_tiles[unit] = grouped

        def quantise(unit):
            codes = cpool.tile([P, NCOL], U32, align_bytes=64, name="codes", tag="codes")
            scales = cpool.tile([P, NCOL], U8, align_bytes=64, name="scales", tag="scales")
            nc.vector.quantize_mx(out=codes[:].bitcast(FP8X4), scales=scales[:], in_=grouped_tiles[unit][:])
            code_tiles[unit] = (codes, scales)

        def multiply(unit):
            h = unit % HEADS
            codes, scales = code_tiles[unit]
            us = []
            for j in range(2):
                cb = h * 2 + j
                acc = psum_a.tile([P, NCOL], F32, name="acc", tag="acc")
                nc.tensor.matmul_mx(
                    out=acc[:],
                    lhsT=w_codes[:, cb * P : (cb + 1) * P].bitcast(FP8X4),
                    lhsT_scale=w_scales[:, cb * P : (cb + 1) * P],
                    rhs=codes[:].bitcast(FP8X4),
                    rhs_scale=scales[:],
                    start=True,
                    stop=True,
                )
                u_sb = upool.tile([P, NCOL], F32, name="u_sb", tag="u")
                nc.scalar.activation(
                    out=u_sb[:], in_=acc[:], func=ACT.Identity, bias=bias_col[:, cb : cb + 1], scale=1.0
                )
                us.append(u_sb)
            u_tiles[unit] = us

        def transpose_back(unit):
            g, h = divmod(unit, HEADS)
            us = u_tiles[unit]
            tbs = []
            for pair in range(2):
                tb = psum_b.tile([P, 2, DH], F32, name="tb", tag="tb")
                for n2 in range(2):
                    n = pair * 2 + n2
                    if pe_adds(unit, pair):
                        nc.tensor.matmul(
                            out=tb[:, n2, :],
                            lhsT=ident_bf[:],
                            rhs=s_all[:, g * GT + n, h * DH : (h + 1) * DH],
                            start=True,
                            stop=False,
                        )
                        for j in range(2):
                            nc.tensor.matmul(
                                out=tb[:, n2, j * P : (j + 1) * P],
                                lhsT=us[j][:, n * P : (n + 1) * P],
                                rhs=ident[:],
                                is_transpose=True,
                                start=False,
                                stop=(j == 1),
                            )
                    else:
                        for j in range(2):
                            nc.tensor.transpose(tb[:, n2, j * P : (j + 1) * P], us[j][:, n * P : (n + 1) * P], ident[:])
                tbs.append(tb)
            tb_tiles[unit] = tbs

        def finish(unit):
            g, h = divmod(unit, HEADS)
            o = xo[:, g * GT : (g + 1) * GT, :]
            s = s_all[:, g * GT : (g + 1) * GT, :]
            v = v_all[:, g * GT : (g + 1) * GT, :]
            cols = slice(h * DH, (h + 1) * DH)
            tbs = tb_tiles[unit]
            plain = [pair for pair in range(2) if not pe_adds(unit, pair)]
            for pair in plain:
                rows = slice(pair * 2, pair * 2 + 2)
                nc.vector.tensor_tensor(out=o[:, rows, cols], in0=tbs[pair][:], in1=s[:, rows, cols], op=ALU.add)
            for pair in range(2):
                rows = slice(pair * 2, pair * 2 + 2)
                nc.vector.scalar_tensor_tensor(
                    out=o[:, rows, cols], in0=o[:, rows, cols] if pair in plain else tbs[pair][:], scalar=0.0,
                    in1=v[:, rows, cols], op0=ALU.max, op1=ALU.add,
                )
                if unit == UNITS - 1:
                    nc.sync.dma_start(out=rows_of(out, g, g + 1)[:, rows, :], in_=o[:, rows, :])
            for g0, g1 in OUT_CHUNKS:
                if h == HEADS - 1 and g == g1 - 1:
                    nc.sync.dma_start(out=rows_of(out, g0, g1), in_=xo[:, g0 * GT : g1 * GT, :])

        wraw = const.tile([P, HEADS, 4, DH], BF16)
        bz = const.tile([P, P], BF16)
        nc.vector.memset(bz[:], 0.0)
        for kind, g0, g1 in LOAD_ORDER:
            load(kind, g0, g1)

        split_words(1)
        wg = const.tile([P, HEADS, DH, 4], BF16, align_bytes=64)
        w_codes = const.tile([P, HEADS * DH], U32, align_bytes=64)
        w_scales = const.tile([P, HEADS * DH], U8, align_bytes=64)
        for h in range(HEADS):
            nc.vector.tensor_copy(out=wg[:, h], in_=wraw[:, h].rearrange("q t c -> q c t"))
            nc.vector.quantize_mx(
                out=w_codes[:, h * DH : (h + 1) * DH].bitcast(FP8X4),
                scales=w_scales[:, h * DH : (h + 1) * DH],
                in_=wg[:, h].rearrange("q c t -> q (c t)"),
            )
        bzf = const.tile([P, P], F32)
        bias_col = const.tile([P, 4], F32)

        for step in range(UNITS + 3):
            if step < UNITS:
                transpose_in(step)
            if step == 1:
                nc.vector.tensor_copy(out=bzf[:], in_=bz[:])
                bt = psum_b.tile([P, P], F32, name="bt", tag="tb")
                nc.tensor.transpose(bt[:], bzf[:], ident[:])
                nc.vector.tensor_copy(out=bias_col[:], in_=bt[:, 0:4])
            if 0 <= step - 1 < UNITS:
                quantise(step - 1)
                if step + 1 in SPLIT_UNITS:
                    split_words(step + 1)
                multiply(step - 1)
            if 0 <= step - 2 < UNITS:
                transpose_back(step - 2)
            if 0 <= step - 3 < UNITS:
                finish(step - 3)
